import numpy as np
import ml_dtypes


def mxq(x, axis, fmt="e4m3"):
    dtype, down = {"e4m3": (ml_dtypes.float8_e4m3fn, 7), "e5m2": (ml_dtypes.float8_e5m2, 14)}[fmt]
    v = np.moveaxis(np.asarray(x, np.float32).astype(ml_dtypes.bfloat16).astype(np.float64), axis, -1)
    blocks = v.reshape(v.shape[:-1] + (-1, 32))
    amax = np.abs(blocks).max(-1, keepdims=True)
    byte = np.maximum(np.where(amax > 0, np.frexp(amax)[1] - 1 + 127, 0) - down, 1)
    scale = np.exp2(byte - 127.0)
    codes = (blocks / scale).astype(np.float32).astype(dtype).astype(np.float64)
    return np.moveaxis((codes * scale).reshape(v.shape), -1, axis)


WIDE = False


def mx_kscale(k):
    if not WIDE:
        return np.ones(k)
    levels = np.array([10, -10, 5, -5, 0])
    if k % 512:
        return np.exp2(np.random.permutation(np.resize(levels, k // 32))).repeat(32)
    a = np.empty((k // 512, 16))
    for p in range(k // 512):
        a[p, :8] = np.random.permutation(np.resize(levels, 8))
        for g in range(8):
            far = levels[np.abs(levels - a[p, g]) >= 10]
            a[p, g + 8] = far[np.random.randint(len(far))]
    return np.exp2(a.ravel()).repeat(32)


BF16 = ml_dtypes.bfloat16


def bf(x):
    return np.asarray(x, np.float32).astype(BF16)


def f64(x):
    return np.asarray(x).astype(np.float64)


B, S, D, H, DH, DR, DKV, DQ = 2, 4096, 512, 2, 128, 64, 512, 1024
HALF = DR // 2


def rope(t, cos, sin):
    t1, t2 = t[..., 0::2], t[..., 1::2]
    c = cos[None, :, None, :]
    s = sin[None, :, None, :]
    return np.stack([t1 * c - t2 * s, t1 * s + t2 * c], axis=-1).reshape(t.shape)


def draw0():
    s, t = mx_kscale(D), mx_kscale(DKV)
    ang = np.random.uniform(0.0, 2.0 * np.pi, (S, HALF))
    return {"x": bf(np.random.standard_normal((B, S, D)) * s),
            "W_kv_down": bf(np.random.standard_normal((D, DKV)) / np.sqrt(D) / s[:, None] * t),
            "W_k_up": bf(np.random.standard_normal((DKV, H * DH)) / np.sqrt(DKV) / t[:, None]),
            "W_v_up": bf(np.random.standard_normal((DKV, H * DH)) / np.sqrt(DKV) / t[:, None]),
            "W_k_rope": bf(np.random.standard_normal((D, H * DR)) / np.sqrt(D) / s[:, None]),
            "rope_cos": bf(np.cos(ang)), "rope_sin": bf(np.sin(ang))}


def core(x, W_kv_down, W_k_up, W_v_up, W_k_rope, rope_cos, rope_sin):
    xq = mxq(f64(x), 2, "e4m3")
    down_kv = xq @ mxq(f64(W_kv_down), 0, "e4m3")
    dkv = mxq(down_kv, 2, "e4m3")
    k_c = (dkv @ mxq(f64(W_k_up), 0, "e4m3")).reshape(B, S, H, DH)
    v = (dkv @ mxq(f64(W_v_up), 0, "e4m3")).reshape(B, S, H, DH)
    k_r = (xq @ mxq(f64(W_k_rope), 0, "e4m3")).reshape(B, S, H, DR)
    k_r = rope(k_r, f64(rope_cos), f64(rope_sin))
    k = np.concatenate([k_c, k_r], axis=-1).transpose(0, 2, 1, 3)
    return k, v.transpose(0, 2, 1, 3)


def e4m3fn_bytes(y):
    return np.clip(np.asarray(y, np.float64), -448.0, 448.0).astype(np.float32).astype(ml_dtypes.float8_e4m3fn).view(np.uint8)


def e4m3fn_values(b):
    return np.asarray(b, np.uint8).view(ml_dtypes.float8_e4m3fn).astype(np.float64)


def setup_inputs():
    d = draw0()
    x0 = np.asarray(d['x']).astype(np.float64)
    s = (np.max(np.abs(x0), axis=(0, 1), keepdims=True) / 448.0).astype(np.float32)
    out = {}
    for k, v in d.items():
        if k == 'x':
            out['x_bytes'] = e4m3fn_bytes(x0 / s.astype(np.float64))
            out['x_scale'] = s
        else:
            out[k] = v
    return out


def reference(x_bytes, x_scale, W_kv_down, W_k_up, W_v_up, W_k_rope, rope_cos, rope_sin):
    return core(e4m3fn_values(x_bytes) * x_scale.astype(np.float64), W_kv_down, W_k_up, W_v_up, W_k_rope, rope_cos, rope_sin)

@@ -1,0 +1,316 @@
+from contextlib import ExitStack
+
+import concourse.mybir as mybir
+from concourse.masks import make_identity
+
+F32 = mybir.dt.float32
+BF16 = mybir.dt.bfloat16
+U32 = mybir.dt.uint32
+U8 = mybir.dt.uint8
+FP8 = mybir.dt.float8_e4m3fn
+FP8X4 = mybir.dt.float8_e4m3fn_x4
+MULT = mybir.AluOpType.mult
+ADD = mybir.AluOpType.add
+
+FLOPS = 2 * 8192 * 512 * (512 + 512 + 128)
+
+P = 128
+GROUPS = 16
+
+
+def tile_multiheadlatentattention_pb_t_kernel(
+    tc, x_bytes, x_scale, w_down, w_kup, w_vup, w_rope, rope_cos, rope_sin, out_0, out_1
+):
+    nc = tc.nc
+    with ExitStack() as ctx:
+        keep = ctx.enter_context(tc.tile_pool(name="keep", bufs=1))
+        bytes_pool = ctx.enter_context(tc.tile_pool(name="bytes_pool", bufs=6))
+        work = ctx.enter_context(tc.tile_pool(name="work", bufs=3))
+        outs = ctx.enter_context(tc.tile_pool(name="outs", bufs=3))
+        ps_x = ctx.enter_context(tc.psum_pool(name="ps_x", bufs=2))
+        ps_1 = ctx.enter_context(tc.psum_pool(name="ps_1", bufs=2))
+        ps_r = ctx.enter_context(tc.psum_pool(name="ps_r", bufs=1))
+        ps_2 = ctx.enter_context(tc.psum_pool(name="ps_2", bufs=3))
+        ctx.enter_context(tc.manual_schedule())
+
+        def tokens(g):
+            b, first = g % 2, 512 * (g // 2)
+            return b, slice(first, first + 512)
+
+        xraw, codes, xg, xq, dg, dq, kr, kt, vt, xt = {}, {}, {}, {}, {}, {}, {}, {}, {}, {}
+        ras, rbs = {}, {}
+
+        def load(g):
+            b, rows = tokens(g)
+            x_raw = bytes_pool.tile([P, 2048], U8, name="x_raw", align_bytes=64)
+            nc.sync.dma_start(out=x_raw[:], in_=x_bytes[b, rows, :].rearrange("(p j) d -> p (j d)", j=4))
+            xraw[g] = x_raw
+
+        load(0)
+        s4 = keep.tile([P, 4], F32, name="s4")
+        nc.sync.dma_start(out=s4[:], in_=x_scale.rearrange("a b (p t) -> p (a b t)", t=4))
+        wd_raw = keep.tile([P, 4, 512], BF16, name="wd_raw")
+        nc.sync.dma_start(out=wd_raw[:], in_=w_down.rearrange("(p j) c -> p j c", j=4))
+        load(1)
+        wr_raw = keep.tile([P, 4, 128], BF16, name="wr_raw")
+        nc.sync.dma_start(out=wr_raw[:], in_=w_rope.rearrange("(p j) c -> p j c", j=4))
+        wk_raw = keep.tile([P, 4, 256], BF16, name="wk_raw")
+        nc.sync.dma_start(out=wk_raw[:], in_=w_kup.rearrange("(p j) c -> p j c", j=4))
+        wv_raw = keep.tile([P, 4, 256], BF16, name="wv_raw")
+        nc.sync.dma_start(out=wv_raw[:], in_=w_vup.rearrange("(p j) c -> p j c", j=4))
+        cos_raw = keep.tile([P, 8, 128], BF16, name="cos_raw")
+        nc.sync.dma_start(out=cos_raw[:], in_=rope_cos.rearrange("(g p j) i -> p g (j i)", p=P, j=4))
+        sin_raw = keep.tile([P, 8, 128], BF16, name="sin_raw")
+        nc.sync.dma_start(out=sin_raw[:], in_=rope_sin.rearrange("(g p j) i -> p g (j i)", p=P, j=4))
+        load(2)
+        load(3)
+
+        ident = keep.tile([P, P], F32, name="ident")
+        make_identity(nc, ident[:])
+        pair_ones = keep.tile([P, 2], BF16, name="pair_ones")
+        nc.gpsimd.memset(pair_ones[:], 1.0)
+        pair_sign = keep.tile([P, 2], BF16, name="pair_sign")
+        nc.gpsimd.memset(pair_sign[:, 0:1], -1.0)
+        nc.gpsimd.memset(pair_sign[:, 1:2], 1.0)
+        cos2 = keep.tile([P, 8, 128, 2], BF16, name="cos2")
+        sin2 = keep.tile([P, 8, 128, 2], BF16, name="sin2")
+
+        def tables(gg):
+            for raw, pair, table in ((cos_raw, pair_ones, cos2), (sin_raw, pair_sign, sin2)):
+                nc.gpsimd.tensor_tensor(
+                    out=table[:, gg],
+                    in0=raw[:, gg].unsqueeze(2).to_broadcast([P, 128, 2]),
+                    in1=pair[:].unsqueeze(1).to_broadcast([P, 128, 2]),
+                    op=MULT,
+                )
+
+        wd_grouped = keep.tile([P, 2048], BF16, name="wd_grouped", align_bytes=64)
+        wu_grouped = keep.tile([P, 2048], BF16, name="wu_grouped", align_bytes=64)
+        wr_grouped = keep.tile([P, 512], BF16, name="wr_grouped", align_bytes=64)
+        wd_q = keep.tile([P, 512], U32, name="wd_q", align_bytes=64)
+        wd_s = keep.tile([P, 512], U8, name="wd_s", align_bytes=64)
+        wu_q = keep.tile([P, 512], U32, name="wu_q", align_bytes=64)
+        wu_s = keep.tile([P, 512], U8, name="wu_s", align_bytes=64)
+        wr_q = keep.tile([P, 128], U32, name="wr_q", align_bytes=64)
+        wr_s = keep.tile([P, 128], U8, name="wr_s", align_bytes=64)
+
+        def cast(g, a):
+            if g not in codes:
+                x_bf = work.tile([P, 2048], BF16, name="x_bf", align_bytes=64, bufs=4)
+                codes[g] = x_bf
+            cols = slice(512 * a, 512 * (a + 1))
+            src = xraw[g][:, cols].bitcast(FP8)
+            engine = cast_engine(g, a)
+            if engine == "v":
+                nc.vector.tensor_copy(out=codes[g][:, cols], in_=src)
+            elif engine == "s":
+                nc.scalar.copy(out=codes[g][:, cols], in_=src)
+            else:
+                nc.gpsimd.tensor_copy(out=codes[g][:, cols], in_=src)
+
+        def cast_engine(g, a):
+            return "v" if g == 0 else "g"
+
+        def turn(g, half):
+            bank = ps_x.tile([P, 2, 256], F32, name="x_bank")
+            words = codes[g][:].bitcast(F32)
+            for i in range(2):
+                a = 2 * half + i
+                for u in range(2):
+                    nc.tensor.transpose(bank[:, u, 128 * i : 128 * (i + 1)], words[:, 256 * a + u : 256 * (a + 1) : 2], ident[:])
+            xt[g, half] = bank
+
+        def product(g, half):
+            if g not in xg:
+                x_grouped = work.tile([P, 2048], BF16, name="x_grouped", align_bytes=64, bufs=2)
+                xg[g] = x_grouped
+            nc.vector.tensor_tensor(
+                out=xg[g][:, 1024 * half : 1024 * (half + 1)].rearrange("p (r u e) -> p r u e", u=2, e=2),
+                in0=xt[g, half][:].bitcast(BF16).rearrange("p u (r e) -> p r u e", e=2),
+                in1=s4[:].rearrange("p (u e) -> p u e", e=2).unsqueeze(1).to_broadcast([P, 256, 2, 2]),
+                op=MULT,
+            )
+
+        def quant(src, name):
+            q = work.tile([P, 512], U32, name=name + "_q", align_bytes=64, bufs=3)
+            s = work.tile([P, 512], U8, name=name + "_s", align_bytes=64, bufs=3)
+            nc.vector.quantize_mx(out=q[:].bitcast(FP8X4), scales=s[:], in_=src[:])
+            return q, s
+
+        def mm(out, lhs, lcols, rhs, rcols):
+            nc.tensor.matmul_mx(
+                out=out,
+                lhsT=lhs[0][:, lcols].bitcast(FP8X4),
+                lhsT_scale=lhs[1][:, lcols],
+                rhs=rhs[0][:, rcols].bitcast(FP8X4),
+                rhs_scale=rhs[1][:, rcols],
+                start=True,
+                stop=True,
+            )
+
+        def tok(a):
+            return slice(128 * a, 128 * (a + 1))
+
+        def copy_out(on_vector, out, in_):
+            if on_vector:
+                nc.vector.tensor_copy(out=out, in_=in_)
+            else:
+                nc.scalar.copy(out=out, in_=in_)
+
+        def down(g, a):
+            if g not in dg:
+                d_grouped = work.tile([P, 2048], BF16, name="d_grouped", align_bytes=64, bufs=2)
+                dg[g] = d_grouped
+            bank = ps_1.tile([P, 4, 128], F32, name="d_bank")
+            for t in range(4):
+                mm(bank[:, t, :], (wd_q, wd_s), tok(t), xq[g], tok(a))
+            copy_out(
+                g == GROUPS - 1 and a % 2 == 1,
+                dg[g][:, 512 * a : 512 * (a + 1)].rearrange("p (n t) -> p n t", t=4),
+                bank[:].rearrange("p t n -> p n t"),
+            )
+
+        def rope_mm(g):
+            bank = ps_r.tile([P, 512], F32, name="r_bank")
+            for a in range(4):
+                mm(bank[:, tok(a)], xq[g], tok(a), (wr_q, wr_s), slice(0, 128))
+            kr[g] = bank
+
+        def rope_a(g):
+            if g not in kt:
+                out_tiles(g)
+            ra = work.tile([P, 512], F32, name="ra", bufs=2)
+            nc.vector.tensor_tensor(
+                out=ra[:].rearrange("p (j h d) -> p j h d", j=4, h=2),
+                in0=kr[g][:].rearrange("p (j h d) -> p j h d", j=4, h=2),
+                in1=cos2[:, g // 2].rearrange("p (j i) o -> p j (i o)", j=4).unsqueeze(2).to_broadcast([P, 4, 2, 64]),
+                op=MULT,
+            )
+            ras[g] = ra
+            if g in rbs:
+                rope_add(g)
+
+        def rope_b(g):
+            if g not in kt:
+                out_tiles(g)
+            rb = work.tile([P, 512], F32, name="rb", bufs=2)
+            nc.vector.tensor_tensor(
+                out=rb[:].rearrange("p (j h i o) -> p j h i o", j=4, h=2, o=2),
+                in0=kr[g][:].rearrange("p (j h i o) -> p j h i o", j=4, h=2, o=2)[:, :, :, :, ::-1],
+                in1=sin2[:, g // 2].rearrange("p (j i) o -> p j i o", j=4).unsqueeze(2).to_broadcast([P, 4, 2, 32, 2]),
+                op=MULT,
+            )
+            rbs[g] = rb
+            if g in ras:
+                rope_add(g)
+
+        def out_tiles(g):
+            k_out = outs.tile([P, 2, 4, 192], F32, name="k_out")
+            v_out = outs.tile([P, 2, 4, 128], F32, name="v_out")
+            kt[g], vt[g] = k_out, v_out
+
+        def rope_add(g):
+            ra, rb = ras[g], rbs[g]
+            engine = nc.vector if g == GROUPS - 1 else nc.gpsimd
+            engine.tensor_tensor(
+                out=kt[g][:, :, :, 128:192],
+                in0=ra[:].rearrange("p (j h d) -> p h j d", j=4, h=2),
+                in1=rb[:].rearrange("p (j h d) -> p h j d", j=4, h=2),
+                op=ADD,
+            )
+
+        def up(g, i):
+            if g not in kt:
+                out_tiles(g)
+            half = i // 2
+            first, dest = ((0, kt[g]), (256, vt[g]))[i % 2]
+            bank = ps_2.tile([P, 2, 256], F32, name="u_bank")
+            for j in range(2):
+                mm(bank[:, j, :], dq[g], tok(2 * half + j), (wu_q, wu_s), slice(first, first + 256))
+            copy_out(
+                g == GROUPS - 1 and i % 2 == 1,
+                dest[:, :, 2 * half : 2 * half + 2, 0:128].rearrange("p h j d -> p j h d"),
+                bank[:].rearrange("p j (h d) -> p j h d", h=2),
+            )
+
+        def store(g):
+            b, rows = tokens(g)
+            keys = out_0[b, :, rows, :].rearrange("h (p j) d -> p h j d", j=4)
+            values = out_1[b, :, rows, :].rearrange("h (p j) d -> p h j d", j=4)
+            if g < GROUPS - 1:
+                nc.sync.dma_start(out=keys.rearrange("p h j d -> p h (j d)"), in_=kt[g][:].rearrange("p h j d -> p h (j d)"))
+                nc.sync.dma_start(out=values.rearrange("p h j d -> p h (j d)"), in_=vt[g][:].rearrange("p h j d -> p h (j d)"))
+            else:
+                for i in last_order:
+                    dest, src = ((keys, kt[g]), (values, vt[g]))[i % 2]
+                    js = slice(2 * (i // 2), 2 * (i // 2) + 2)
+                    nc.sync.dma_start(
+                        out=dest[:, :, js, :].rearrange("p h j d -> p h (j d)"),
+                        in_=src[:, :, js, :].rearrange("p h j d -> p h (j d)"),
+                    )
+
+        last_order = [2,3,1,0]
+
+        def quant_x(g):
+            if g == 0:
+                nc.vector.quantize_mx(out=wd_q[:].bitcast(FP8X4), scales=wd_s[:], in_=wd_grouped[:])
+                nc.vector.tensor_copy(out=wr_grouped[:].rearrange("p (c j) -> p c j", j=4), in_=wr_raw[:].rearrange("p j c -> p c j"))
+            xq[g] = quant(xg[g], "x")
+            if g == 0:
+                nc.vector.quantize_mx(out=wr_q[:].bitcast(FP8X4), scales=wr_s[:], in_=wr_grouped[:])
+
+        def quant_d(g):
+            if g == 0:
+                nc.vector.quantize_mx(out=wu_q[:].bitcast(FP8X4), scales=wu_s[:], in_=wu_grouped[:])
+            dq[g] = quant(dg[g], "d")
+
+        nc.scalar.copy(out=wd_grouped[:].rearrange("p (t m j) -> p t m j", t=4, j=4), in_=wd_raw[:].rearrange("p j (m t) -> p t m j", t=4))
+        nc.scalar.copy(out=wu_grouped[:, 0:1024].rearrange("p (c j) -> p c j", j=4), in_=wk_raw[:].rearrange("p j c -> p c j"))
+        nc.scalar.copy(out=wu_grouped[:, 1024:2048].rearrange("p (c j) -> p c j", j=4), in_=wv_raw[:].rearrange("p j c -> p c j"))
+        stages = {
+            "L": lambda g: load(g) if g >= 4 else None,
+            "TB": lambda g: tables(g // 2) if g % 2 == 0 else None,
+            "Q1": quant_x,
+            "R": rope_mm,
+            "A": rope_a,
+            "B": rope_b,
+            "Q2": quant_d,
+            "ST": store,
+        }
+        for a in range(4):
+            stages["C" + str(a)] = lambda g, a=a: cast(g, a)
+            stages["D" + str(a)] = lambda g, a=a: down(g, a)
+            stages["U" + str(a)] = lambda g, a=a: up(g, a)
+        for h in range(2):
+            stages["T" + str(h)] = lambda g, h=h: turn(g, h)
+            stages["P" + str(h)] = lambda g, h=h: product(g, h)
+        frame = [
+            ("L", -6),
+            ("D2", 0),
+            ("C1", -3),
+            ("B", 1),
+            ("U3", 1),
+            ("ST", 3),
+            ("D1", -1),
+            ("U1", 1),
+            ("R", 0),
+            ("P0", -2),
+            ("A", 0),
+            ("Q2", 0),
+            ("T1", -2),
+            ("TB", -3),
+            ("C0", -3),
+            ("P1", -2),
+            ("Q1", -2),
+            ("C3", -3),
+            ("D0", -1),
+            ("U0", 1),
+            ("D3", -1),
+            ("U2", 0),
+            ("C2", -3),
+            ("T0", -3),
+        ]
+        for f in range(-6, 20):
+            for name, lag in frame:
+                if 0 <= f - lag < GROUPS:
+                    stages[name](f - lag)

@@ -17,6 +17,40 @@ FLOPS = 2 * 8192 * 512 * (512 + 512 + 128)
 P = 128
 GROUPS = 16
 
+FRAME = (
+    ("X1", -3),
+    ("D0", -1),
+    ("LOAD", -6),
+    ("D1", -1),
+    ("Q2", 0),
+    ("U2", 1),
+    ("AD", 1),
+    ("U3", 1),
+    ("P1", -4),
+    ("Q1", -2),
+    ("R", 0),
+    ("D2", -1),
+    ("D3", -1),
+    ("U0", 0),
+    ("B", 0),
+    ("ST", 2),
+    ("U1", 0),
+    ("T0", -3),
+    ("A", 0),
+    ("T1", -4),
+    ("P0", -4),
+    ("X0", -3),
+)
+ON_VECTOR = {
+    1: ("U1",),
+    5: ("U2",),
+    6: ("U0",),
+    9: ("D3",),
+    12: ("U0", "U2",),
+    13: ("U2",),
+    15: ("X1", "D2", "U3",),
+}
+
 
 def tile_multiheadlatentattention_pb_t_kernel(
     tc, x_bytes, x_scale, w_down, w_kup, w_vup, w_rope, rope_cos, rope_sin, out_0, out_1
@@ -24,31 +58,33 @@ def tile_multiheadlatentattention_pb_t_kernel(
     nc = tc.nc
     with ExitStack() as ctx:
         keep = ctx.enter_context(tc.tile_pool(name="keep", bufs=1))
-        bytes_pool = ctx.enter_context(tc.tile_pool(name="bytes_pool", bufs=6))
         work = ctx.enter_context(tc.tile_pool(name="work", bufs=3))
-        outs = ctx.enter_context(tc.tile_pool(name="outs", bufs=3))
         ps_x = ctx.enter_context(tc.psum_pool(name="ps_x", bufs=2))
-        ps_1 = ctx.enter_context(tc.psum_pool(name="ps_1", bufs=2))
+        ps_d = ctx.enter_context(tc.psum_pool(name="ps_d", bufs=2))
         ps_r = ctx.enter_context(tc.psum_pool(name="ps_r", bufs=1))
-        ps_2 = ctx.enter_context(tc.psum_pool(name="ps_2", bufs=3))
+        ps_u = ctx.enter_context(tc.psum_pool(name="ps_u", bufs=3))
         ctx.enter_context(tc.manual_schedule())
 
-        def tokens(g):
-            b, first = g % 2, 512 * (g // 2)
-            return b, slice(first, first + 512)
+        def rows_of(g):
+            first = 512 * (g // 2)
+            return g % 2, slice(first, first + 512)
 
-        xraw, codes, xg, xq, dg, dq, kr, kt, vt, xt = {}, {}, {}, {}, {}, {}, {}, {}, {}, {}
-        ras, rbs = {}, {}
+        x_fp8, x_bf, x_bank, x_grouped, xq = {}, {}, {}, {}, {}
+        d_grouped, dq, r_bank, r_cos, r_sin, k_out, v_out = {}, {}, {}, {}, {}, {}, {}
+
+        def tile_of(table, g, *args, **kwargs):
+            if g not in table:
+                table[g] = work.tile(*args, **kwargs)
+            return table[g]
 
         def load(g):
-            b, rows = tokens(g)
-            x_raw = bytes_pool.tile([P, 2048], U8, name="x_raw", align_bytes=64)
-            nc.sync.dma_start(out=x_raw[:], in_=x_bytes[b, rows, :].rearrange("(p j) d -> p (j d)", j=4))
-            xraw[g] = x_raw
+            b, rows = rows_of(g)
+            t = tile_of(x_fp8, g, [P, 2048], U8, name="x_fp8", align_bytes=64, bufs=6)
+            nc.sync.dma_start(out=t[:], in_=x_bytes[b, rows, :].rearrange("(p j) d -> p (j d)", j=4))
 
         load(0)
-        s4 = keep.tile([P, 4], F32, name="s4")
-        nc.sync.dma_start(out=s4[:], in_=x_scale.rearrange("a b (p t) -> p (a b t)", t=4))
+        scale2 = keep.tile([P, 1024], F32, name="scale2")
+        nc.sync.dma_start(out=scale2[:, 0:512], in_=x_scale.rearrange("a b k -> (a b k)").partition_broadcast(P))
         wd_raw = keep.tile([P, 4, 512], BF16, name="wd_raw")
         nc.sync.dma_start(out=wd_raw[:], in_=w_down.rearrange("(p j) c -> p j c", j=4))
         load(1)
@@ -58,259 +94,189 @@ def tile_multiheadlatentattention_pb_t_kernel(
         nc.sync.dma_start(out=wk_raw[:], in_=w_kup.rearrange("(p j) c -> p j c", j=4))
         wv_raw = keep.tile([P, 4, 256], BF16, name="wv_raw")
         nc.sync.dma_start(out=wv_raw[:], in_=w_vup.rearrange("(p j) c -> p j c", j=4))
-        cos_raw = keep.tile([P, 8, 128], BF16, name="cos_raw")
-        nc.sync.dma_start(out=cos_raw[:], in_=rope_cos.rearrange("(g p j) i -> p g (j i)", p=P, j=4))
-        sin_raw = keep.tile([P, 8, 128], BF16, name="sin_raw")
-        nc.sync.dma_start(out=sin_raw[:], in_=rope_sin.rearrange("(g p j) i -> p g (j i)", p=P, j=4))
+        cos_rows = keep.tile([P, 8, 128], BF16, name="cos_rows")
+        nc.sync.dma_start(out=cos_rows[:], in_=rope_cos.rearrange("(g p j) i -> p g (j i)", p=P, j=4))
+        sin_rows = keep.tile([P, 8, 128], BF16, name="sin_rows")
+        nc.sync.dma_start(out=sin_rows[:], in_=rope_sin.rearrange("(g p j) i -> p g (j i)", p=P, j=4))
         load(2)
-        load(3)
 
         ident = keep.tile([P, P], F32, name="ident")
         make_identity(nc, ident[:])
-        pair_ones = keep.tile([P, 2], BF16, name="pair_ones")
-        nc.gpsimd.memset(pair_ones[:], 1.0)
-        pair_sign = keep.tile([P, 2], BF16, name="pair_sign")
-        nc.gpsimd.memset(pair_sign[:, 0:1], -1.0)
-        nc.gpsimd.memset(pair_sign[:, 1:2], 1.0)
-        cos2 = keep.tile([P, 8, 128, 2], BF16, name="cos2")
-        sin2 = keep.tile([P, 8, 128, 2], BF16, name="sin2")
-
-        def tables(gg):
-            for raw, pair, table in ((cos_raw, pair_ones, cos2), (sin_raw, pair_sign, sin2)):
-                nc.gpsimd.tensor_tensor(
-                    out=table[:, gg],
-                    in0=raw[:, gg].unsqueeze(2).to_broadcast([P, 128, 2]),
-                    in1=pair[:].unsqueeze(1).to_broadcast([P, 128, 2]),
-                    op=MULT,
-                )
+        sin2 = keep.tile([P, 32, 2, 32], BF16, name="sin2")
 
         wd_grouped = keep.tile([P, 2048], BF16, name="wd_grouped", align_bytes=64)
         wu_grouped = keep.tile([P, 2048], BF16, name="wu_grouped", align_bytes=64)
         wr_grouped = keep.tile([P, 512], BF16, name="wr_grouped", align_bytes=64)
-        wd_q = keep.tile([P, 512], U32, name="wd_q", align_bytes=64)
-        wd_s = keep.tile([P, 512], U8, name="wd_s", align_bytes=64)
-        wu_q = keep.tile([P, 512], U32, name="wu_q", align_bytes=64)
-        wu_s = keep.tile([P, 512], U8, name="wu_s", align_bytes=64)
-        wr_q = keep.tile([P, 128], U32, name="wr_q", align_bytes=64)
-        wr_s = keep.tile([P, 128], U8, name="wr_s", align_bytes=64)
+        wd = (keep.tile([P, 512], U32, name="wd_q", align_bytes=64), keep.tile([P, 512], U8, name="wd_s", align_bytes=64))
+        wu = (keep.tile([P, 512], U32, name="wu_q", align_bytes=64), keep.tile([P, 512], U8, name="wu_s", align_bytes=64))
+        wr = (keep.tile([P, 128], U32, name="wr_q", align_bytes=64), keep.tile([P, 128], U8, name="wr_s", align_bytes=64))
 
-        def cast(g, a):
-            if g not in codes:
-                x_bf = work.tile([P, 2048], BF16, name="x_bf", align_bytes=64, bufs=4)
-                codes[g] = x_bf
-            cols = slice(512 * a, 512 * (a + 1))
-            src = xraw[g][:, cols].bitcast(FP8)
-            engine = cast_engine(g, a)
-            if engine == "v":
-                nc.vector.tensor_copy(out=codes[g][:, cols], in_=src)
-            elif engine == "s":
-                nc.scalar.copy(out=codes[g][:, cols], in_=src)
-            else:
-                nc.gpsimd.tensor_copy(out=codes[g][:, cols], in_=src)
+        def quantize(pair, src):
+            nc.vector.quantize_mx(out=pair[0][:].bitcast(FP8X4), scales=pair[1][:], in_=src[:])
 
-        def cast_engine(g, a):
-            return "v" if g == 0 else "g"
-
-        def turn(g, half):
-            bank = ps_x.tile([P, 2, 256], F32, name="x_bank")
-            words = codes[g][:].bitcast(F32)
-            for i in range(2):
-                a = 2 * half + i
-                for u in range(2):
-                    nc.tensor.transpose(bank[:, u, 128 * i : 128 * (i + 1)], words[:, 256 * a + u : 256 * (a + 1) : 2], ident[:])
-            xt[g, half] = bank
-
-        def product(g, half):
-            if g not in xg:
-                x_grouped = work.tile([P, 2048], BF16, name="x_grouped", align_bytes=64, bufs=2)
-                xg[g] = x_grouped
-            nc.vector.tensor_tensor(
-                out=xg[g][:, 1024 * half : 1024 * (half + 1)].rearrange("p (r u e) -> p r u e", u=2, e=2),
-                in0=xt[g, half][:].bitcast(BF16).rearrange("p u (r e) -> p r u e", e=2),
-                in1=s4[:].rearrange("p (u e) -> p u e", e=2).unsqueeze(1).to_broadcast([P, 256, 2, 2]),
-                op=MULT,
-            )
-
-        def quant(src, name):
-            q = work.tile([P, 512], U32, name=name + "_q", align_bytes=64, bufs=3)
-            s = work.tile([P, 512], U8, name=name + "_s", align_bytes=64, bufs=3)
-            nc.vector.quantize_mx(out=q[:].bitcast(FP8X4), scales=s[:], in_=src[:])
-            return q, s
-
-        def mm(out, lhs, lcols, rhs, rcols):
-            nc.tensor.matmul_mx(
-                out=out,
-                lhsT=lhs[0][:, lcols].bitcast(FP8X4),
-                lhsT_scale=lhs[1][:, lcols],
-                rhs=rhs[0][:, rcols].bitcast(FP8X4),
-                rhs_scale=rhs[1][:, rcols],
-                start=True,
-                stop=True,
-            )
-
-        def tok(a):
-            return slice(128 * a, 128 * (a + 1))
-
-        def copy_out(on_vector, out, in_):
-            if on_vector:
+        def copy_out(name, g, out, in_):
+            if name in ON_VECTOR.get(g, ()):
                 nc.vector.tensor_copy(out=out, in_=in_)
             else:
                 nc.scalar.copy(out=out, in_=in_)
 
-        def down(g, a):
-            if g not in dg:
-                d_grouped = work.tile([P, 2048], BF16, name="d_grouped", align_bytes=64, bufs=2)
-                dg[g] = d_grouped
-            bank = ps_1.tile([P, 4, 128], F32, name="d_bank")
-            for t in range(4):
-                mm(bank[:, t, :], (wd_q, wd_s), tok(t), xq[g], tok(a))
+        def product(g, half):
+            t = tile_of(x_bf, g, [P, 2048], BF16, name="x_bf", align_bytes=64, bufs=3)
+            width = 512 if g == 0 else 1024
+            for first in range(1024 * half, 1024 * (half + 1), width):
+                cols = slice(first, first + width)
+                nc.vector.tensor_tensor(out=t[:, cols], in0=x_fp8[g][:, cols].bitcast(FP8), in1=scale2[:, 0:width], op=MULT)
+
+        def turn(g, half):
+            bank = ps_x.tile([P, 2, 256], F32, name="x_bank")
+            words = x_bf[g][:].bitcast(F32)
+            for i in range(2):
+                a = 2 * half + i
+                for u in range(2):
+                    nc.tensor.transpose(bank[:, u, 128 * i : 128 * (i + 1)], words[:, 256 * a + u : 256 * (a + 1) : 2], ident[:])
+            x_bank[g, half] = bank
+
+        def words_out(g, half):
+            t = tile_of(x_grouped, g, [P, 2048], BF16, name="x_grouped", align_bytes=64, bufs=2)
             copy_out(
-                g == GROUPS - 1 and a % 2 == 1,
-                dg[g][:, 512 * a : 512 * (a + 1)].rearrange("p (n t) -> p n t", t=4),
+                "X" + str(half),
+                g,
+                t[:].bitcast(F32)[:, 512 * half : 512 * (half + 1)].rearrange("p (r u) -> p r u", u=2),
+                x_bank[g, half][:].rearrange("p u r -> p r u"),
+            )
+
+        def quantized(src, name):
+            codes = work.tile([P, 512], U32, name=name + "_codes", align_bytes=64, bufs=3)
+            scales = work.tile([P, 512], U8, name=name + "_scales", align_bytes=64, bufs=3)
+            quantize((codes, scales), src)
+            return codes, scales
+
+        def multiply(out, lhs, lhs_cols, rhs, rhs_cols):
+            nc.tensor.matmul_mx(
+                out=out,
+                lhsT=lhs[0][:, lhs_cols].bitcast(FP8X4),
+                lhsT_scale=lhs[1][:, lhs_cols],
+                rhs=rhs[0][:, rhs_cols].bitcast(FP8X4),
+                rhs_scale=rhs[1][:, rhs_cols],
+                start=True,
+                stop=True,
+            )
+
+        def block(a):
+            return slice(128 * a, 128 * (a + 1))
+
+        def down(g, a):
+            t = tile_of(d_grouped, g, [P, 2048], BF16, name="d_grouped", align_bytes=64, bufs=2)
+            bank = ps_d.tile([P, 4, 128], F32, name="d_bank")
+            for c in range(4):
+                multiply(bank[:, c, :], wd, block(c), xq[g], block(a))
+            copy_out(
+                "D" + str(a),
+                g,
+                t[:, 512 * a : 512 * (a + 1)].rearrange("p (n t) -> p n t", t=4),
                 bank[:].rearrange("p t n -> p n t"),
             )
 
-        def rope_mm(g):
+        def rope_matmul(g):
             bank = ps_r.tile([P, 512], F32, name="r_bank")
             for a in range(4):
-                mm(bank[:, tok(a)], xq[g], tok(a), (wr_q, wr_s), slice(0, 128))
-            kr[g] = bank
+                multiply(bank[:, block(a)], xq[g], block(a), wr, slice(0, 128))
+            r_bank[g] = bank
 
-        def rope_a(g):
-            if g not in kt:
-                out_tiles(g)
-            ra = work.tile([P, 512], F32, name="ra", bufs=2)
+        def rope_cosines(g):
+            t = tile_of(r_cos, g, [P, 2, 4, 64], F32, name="r_cos", bufs=2)
             nc.vector.tensor_tensor(
-                out=ra[:].rearrange("p (j h d) -> p j h d", j=4, h=2),
-                in0=kr[g][:].rearrange("p (j h d) -> p j h d", j=4, h=2),
-                in1=cos2[:, g // 2].rearrange("p (j i) o -> p j (i o)", j=4).unsqueeze(2).to_broadcast([P, 4, 2, 64]),
+                out=t[:].rearrange("p h j (i o) -> p h j i o", o=2),
+                in0=r_bank[g][:].rearrange("p (j h i o) -> p h j i o", j=4, h=2, o=2),
+                in1=cos_rows[:, g // 2].rearrange("p (j i) -> p j i", j=4).unsqueeze(1).unsqueeze(4).to_broadcast([P, 2, 4, 32, 2]),
                 op=MULT,
             )
-            ras[g] = ra
-            if g in rbs:
-                rope_add(g)
 
-        def rope_b(g):
-            if g not in kt:
-                out_tiles(g)
-            rb = work.tile([P, 512], F32, name="rb", bufs=2)
-            nc.vector.tensor_tensor(
-                out=rb[:].rearrange("p (j h i o) -> p j h i o", j=4, h=2, o=2),
-                in0=kr[g][:].rearrange("p (j h i o) -> p j h i o", j=4, h=2, o=2)[:, :, :, :, ::-1],
-                in1=sin2[:, g // 2].rearrange("p (j i) o -> p j i o", j=4).unsqueeze(2).to_broadcast([P, 4, 2, 32, 2]),
-                op=MULT,
-            )
-            rbs[g] = rb
-            if g in ras:
-                rope_add(g)
+        def rope_sines(g):
+            if g == 0:
+                rows = sin_rows[:].rearrange("p g (j i) -> p (g j) i", j=4)
+                nc.vector.tensor_scalar(out=sin2[:, :, 0, :], in0=rows, scalar1=-1.0, scalar2=None, op0=MULT)
+                nc.vector.tensor_copy(out=sin2[:, :, 1, :], in_=rows)
+            t = tile_of(r_sin, g, [P, 2, 4, 64], F32, name="r_sin", bufs=2)
+            first = 4 * (g // 2)
+            for h in range(2):
+                nc.vector.tensor_tensor(
+                    out=t[:, h].rearrange("p j (i o) -> p j i o", o=2),
+                    in0=r_bank[g][:].rearrange("p (j h i o) -> p h j i o", j=4, h=2, o=2)[:, h, :, :, ::-1],
+                    in1=sin2[:, first : first + 4].rearrange("p j o i -> p j i o"),
+                    op=MULT,
+                )
 
-        def out_tiles(g):
-            k_out = outs.tile([P, 2, 4, 192], F32, name="k_out")
-            v_out = outs.tile([P, 2, 4, 128], F32, name="v_out")
-            kt[g], vt[g] = k_out, v_out
+        def keys_of(g):
+            return tile_of(k_out, g, [P, 2, 4, 192], F32, name="k_out", bufs=3)
 
-        def rope_add(g):
-            ra, rb = ras[g], rbs[g]
-            engine = nc.vector if g == GROUPS - 1 else nc.gpsimd
-            engine.tensor_tensor(
-                out=kt[g][:, :, :, 128:192],
-                in0=ra[:].rearrange("p (j h d) -> p h j d", j=4, h=2),
-                in1=rb[:].rearrange("p (j h d) -> p h j d", j=4, h=2),
-                op=ADD,
-            )
+        def values_of(g):
+            return tile_of(v_out, g, [P, 2, 4, 128], F32, name="v_out", bufs=3)
+
+        def rope_sum(g):
+            engine = nc.vector
+            engine.tensor_tensor(out=keys_of(g)[:, :, :, 128:192], in0=r_cos[g][:], in1=r_sin[g][:], op=ADD)
 
         def up(g, i):
-            if g not in kt:
-                out_tiles(g)
             half = i // 2
-            first, dest = ((0, kt[g]), (256, vt[g]))[i % 2]
-            bank = ps_2.tile([P, 2, 256], F32, name="u_bank")
+            first, dest = ((0, keys_of(g)), (256, values_of(g)))[i % 2]
+            bank = ps_u.tile([P, 2, 256], F32, name="u_bank")
             for j in range(2):
-                mm(bank[:, j, :], dq[g], tok(2 * half + j), (wu_q, wu_s), slice(first, first + 256))
+                multiply(bank[:, j, :], dq[g], block(2 * half + j), wu, slice(first, first + 256))
             copy_out(
-                g == GROUPS - 1 and i % 2 == 1,
+                "U" + str(i),
+                g,
                 dest[:, :, 2 * half : 2 * half + 2, 0:128].rearrange("p h j d -> p j h d"),
                 bank[:].rearrange("p j (h d) -> p j h d", h=2),
             )
 
         def store(g):
-            b, rows = tokens(g)
+            b, rows = rows_of(g)
             keys = out_0[b, :, rows, :].rearrange("h (p j) d -> p h j d", j=4)
             values = out_1[b, :, rows, :].rearrange("h (p j) d -> p h j d", j=4)
-            if g < GROUPS - 1:
-                nc.sync.dma_start(out=keys.rearrange("p h j d -> p h (j d)"), in_=kt[g][:].rearrange("p h j d -> p h (j d)"))
-                nc.sync.dma_start(out=values.rearrange("p h j d -> p h (j d)"), in_=vt[g][:].rearrange("p h j d -> p h (j d)"))
-            else:
-                for i in last_order:
-                    dest, src = ((keys, kt[g]), (values, vt[g]))[i % 2]
-                    js = slice(2 * (i // 2), 2 * (i // 2) + 2)
+            parts = ((0, 4),) if g < GROUPS - 1 else ((0, 2), (2, 4))
+            for lo, hi in parts:
+                for dest, src in ((keys, k_out[g]), (values, v_out[g])):
                     nc.sync.dma_start(
-                        out=dest[:, :, js, :].rearrange("p h j d -> p h (j d)"),
-                        in_=src[:, :, js, :].rearrange("p h j d -> p h (j d)"),
+                        out=dest[:, :, lo:hi, :].rearrange("p h j d -> p h (j d)"),
+                        in_=src[:, :, lo:hi, :].rearrange("p h j d -> p h (j d)"),
                     )
 
-        last_order = [2,3,1,0]
-
-        def quant_x(g):
+        def quantize_x(g):
             if g == 0:
-                nc.vector.quantize_mx(out=wd_q[:].bitcast(FP8X4), scales=wd_s[:], in_=wd_grouped[:])
+                quantize(wd, wd_grouped)
+            xq[g] = quantized(x_grouped[g], "x")
+            if g == 0:
                 nc.vector.tensor_copy(out=wr_grouped[:].rearrange("p (c j) -> p c j", j=4), in_=wr_raw[:].rearrange("p j c -> p c j"))
-            xq[g] = quant(xg[g], "x")
-            if g == 0:
-                nc.vector.quantize_mx(out=wr_q[:].bitcast(FP8X4), scales=wr_s[:], in_=wr_grouped[:])
+                nc.vector.tensor_copy(out=wu_grouped[:, 1024:2048].rearrange("p (c j) -> p c j", j=4), in_=wv_raw[:].rearrange("p j c -> p c j"))
+                quantize(wr, wr_grouped)
 
-        def quant_d(g):
+        def quantize_d(g):
             if g == 0:
-                nc.vector.quantize_mx(out=wu_q[:].bitcast(FP8X4), scales=wu_s[:], in_=wu_grouped[:])
-            dq[g] = quant(dg[g], "d")
+                quantize(wu, wu_grouped)
+            dq[g] = quantized(d_grouped[g], "d")
 
+        nc.scalar.copy(out=scale2[:, 512:1024], in_=scale2[:, 0:512])
         nc.scalar.copy(out=wd_grouped[:].rearrange("p (t m j) -> p t m j", t=4, j=4), in_=wd_raw[:].rearrange("p j (m t) -> p t m j", t=4))
         nc.scalar.copy(out=wu_grouped[:, 0:1024].rearrange("p (c j) -> p c j", j=4), in_=wk_raw[:].rearrange("p j c -> p c j"))
-        nc.scalar.copy(out=wu_grouped[:, 1024:2048].rearrange("p (c j) -> p c j", j=4), in_=wv_raw[:].rearrange("p j c -> p c j"))
         stages = {
-            "L": lambda g: load(g) if g >= 4 else None,
-            "TB": lambda g: tables(g // 2) if g % 2 == 0 else None,
-            "Q1": quant_x,
-            "R": rope_mm,
-            "A": rope_a,
-            "B": rope_b,
-            "Q2": quant_d,
+            "LOAD": lambda g: load(g) if g > 2 else None,
+            "Q1": quantize_x,
+            "R": rope_matmul,
+            "A": rope_cosines,
+            "B": rope_sines,
+            "AD": rope_sum,
+            "Q2": quantize_d,
             "ST": store,
         }
-        for a in range(4):
-            stages["C" + str(a)] = lambda g, a=a: cast(g, a)
-            stages["D" + str(a)] = lambda g, a=a: down(g, a)
-            stages["U" + str(a)] = lambda g, a=a: up(g, a)
-        for h in range(2):
-            stages["T" + str(h)] = lambda g, h=h: turn(g, h)
-            stages["P" + str(h)] = lambda g, h=h: product(g, h)
-        frame = [
-            ("L", -6),
-            ("D2", 0),
-            ("C1", -3),
-            ("B", 1),
-            ("U3", 1),
-            ("ST", 3),
-            ("D1", -1),
-            ("U1", 1),
-            ("R", 0),
-            ("P0", -2),
-            ("A", 0),
-            ("Q2", 0),
-            ("T1", -2),
-            ("TB", -3),
-            ("C0", -3),
-            ("P1", -2),
-            ("Q1", -2),
-            ("C3", -3),
-            ("D0", -1),
-            ("U0", 1),
-            ("D3", -1),
-            ("U2", 0),
-            ("C2", -3),
-            ("T0", -3),
-        ]
-        for f in range(-6, 20):
-            for name, lag in frame:
+        for i in range(4):
+            stages["D" + str(i)] = lambda g, i=i: down(g, i)
+            stages["U" + str(i)] = lambda g, i=i: up(g, i)
+        for i in range(2):
+            stages["P" + str(i)] = lambda g, i=i: product(g, i)
+            stages["T" + str(i)] = lambda g, i=i: turn(g, i)
+            stages["X" + str(i)] = lambda g, i=i: words_out(g, i)
+        for f in range(-6, 19):
+            for name, lag in FRAME:
                 if 0 <= f - lag < GROUPS:
                     stages[name](f - lag)

from contextlib import ExitStack

import concourse.mybir as mybir
from concourse.masks import make_identity

F32 = mybir.dt.float32
BF16 = mybir.dt.bfloat16
U32 = mybir.dt.uint32
U8 = mybir.dt.uint8
FP8 = mybir.dt.float8_e4m3fn
FP8X4 = mybir.dt.float8_e4m3fn_x4
MULT = mybir.AluOpType.mult
ADD = mybir.AluOpType.add

FLOPS = 2 * 8192 * 512 * (512 + 512 + 128)

P = 128
GROUPS = 16

FRAME = (
    ("X1", -3),
    ("D0", -1),
    ("LOAD", -6),
    ("D1", -1),
    ("Q2", 0),
    ("U2", 1),
    ("AD", 1),
    ("U3", 1),
    ("P1", -4),
    ("Q1", -2),
    ("R", 0),
    ("D2", -1),
    ("D3", -1),
    ("U0", 0),
    ("B", 0),
    ("ST", 2),
    ("U1", 0),
    ("T0", -3),
    ("A", 0),
    ("T1", -4),
    ("P0", -4),
    ("X0", -3),
)
ON_VECTOR = {
    1: ("U1",),
    5: ("U2",),
    6: ("U0",),
    9: ("D3",),
    12: ("U0", "U2",),
    13: ("U2",),
    15: ("X1", "D2", "U3",),
}


def tile_multiheadlatentattention_pb_t_kernel(
    tc, x_bytes, x_scale, w_down, w_kup, w_vup, w_rope, rope_cos, rope_sin, out_0, out_1
):
    nc = tc.nc
    with ExitStack() as ctx:
        keep = ctx.enter_context(tc.tile_pool(name="keep", bufs=1))
        work = ctx.enter_context(tc.tile_pool(name="work", bufs=3))
        ps_x = ctx.enter_context(tc.psum_pool(name="ps_x", bufs=2))
        ps_d = ctx.enter_context(tc.psum_pool(name="ps_d", bufs=2))
        ps_r = ctx.enter_context(tc.psum_pool(name="ps_r", bufs=1))
        ps_u = ctx.enter_context(tc.psum_pool(name="ps_u", bufs=3))
        ctx.enter_context(tc.manual_schedule())

        def rows_of(g):
            first = 512 * (g // 2)
            return g % 2, slice(first, first + 512)

        x_fp8, x_bf, x_bank, x_grouped, xq = {}, {}, {}, {}, {}
        d_grouped, dq, r_bank, r_cos, r_sin, k_out, v_out = {}, {}, {}, {}, {}, {}, {}

        def tile_of(table, g, *args, **kwargs):
            if g not in table:
                table[g] = work.tile(*args, **kwargs)
            return table[g]

        def load(g):
            b, rows = rows_of(g)
            t = tile_of(x_fp8, g, [P, 2048], U8, name="x_fp8", align_bytes=64, bufs=6)
            nc.sync.dma_start(out=t[:], in_=x_bytes[b, rows, :].rearrange("(p j) d -> p (j d)", j=4))

        load(0)
        scale2 = keep.tile([P, 1024], F32, name="scale2")
        nc.sync.dma_start(out=scale2[:, 0:512], in_=x_scale.rearrange("a b k -> (a b k)").partition_broadcast(P))
        wd_raw = keep.tile([P, 4, 512], BF16, name="wd_raw")
        nc.sync.dma_start(out=wd_raw[:], in_=w_down.rearrange("(p j) c -> p j c", j=4))
        load(1)
        wr_raw = keep.tile([P, 4, 128], BF16, name="wr_raw")
        nc.sync.dma_start(out=wr_raw[:], in_=w_rope.rearrange("(p j) c -> p j c", j=4))
        wk_raw = keep.tile([P, 4, 256], BF16, name="wk_raw")
        nc.sync.dma_start(out=wk_raw[:], in_=w_kup.rearrange("(p j) c -> p j c", j=4))
        wv_raw = keep.tile([P, 4, 256], BF16, name="wv_raw")
        nc.sync.dma_start(out=wv_raw[:], in_=w_vup.rearrange("(p j) c -> p j c", j=4))
        cos_rows = keep.tile([P, 8, 128], BF16, name="cos_rows")
        nc.sync.dma_start(out=cos_rows[:], in_=rope_cos.rearrange("(g p j) i -> p g (j i)", p=P, j=4))
        sin_rows = keep.tile([P, 8, 128], BF16, name="sin_rows")
        nc.sync.dma_start(out=sin_rows[:], in_=rope_sin.rearrange("(g p j) i -> p g (j i)", p=P, j=4))
        load(2)

        ident = keep.tile([P, P], F32, name="ident")
        make_identity(nc, ident[:])
        sin2 = keep.tile([P, 32, 2, 32], BF16, name="sin2")

        wd_grouped = keep.tile([P, 2048], BF16, name="wd_grouped", align_bytes=64)
        wu_grouped = keep.tile([P, 2048], BF16, name="wu_grouped", align_bytes=64)
        wr_grouped = keep.tile([P, 512], BF16, name="wr_grouped", align_bytes=64)
        wd = (keep.tile([P, 512], U32, name="wd_q", align_bytes=64), keep.tile([P, 512], U8, name="wd_s", align_bytes=64))
        wu = (keep.tile([P, 512], U32, name="wu_q", align_bytes=64), keep.tile([P, 512], U8, name="wu_s", align_bytes=64))
        wr = (keep.tile([P, 128], U32, name="wr_q", align_bytes=64), keep.tile([P, 128], U8, name="wr_s", align_bytes=64))

        def quantize(pair, src):
            nc.vector.quantize_mx(out=pair[0][:].bitcast(FP8X4), scales=pair[1][:], in_=src[:])

        def copy_out(name, g, out, in_):
            if name in ON_VECTOR.get(g, ()):
                nc.vector.tensor_copy(out=out, in_=in_)
            else:
                nc.scalar.copy(out=out, in_=in_)

        def product(g, half):
            t = tile_of(x_bf, g, [P, 2048], BF16, name="x_bf", align_bytes=64, bufs=3)
            width = 512 if g == 0 else 1024
            for first in range(1024 * half, 1024 * (half + 1), width):
                cols = slice(first, first + width)
                nc.vector.tensor_tensor(out=t[:, cols], in0=x_fp8[g][:, cols].bitcast(FP8), in1=scale2[:, 0:width], op=MULT)

        def turn(g, half):
            bank = ps_x.tile([P, 2, 256], F32, name="x_bank")
            words = x_bf[g][:].bitcast(F32)
            for i in range(2):
                a = 2 * half + i
                for u in range(2):
                    nc.tensor.transpose(bank[:, u, 128 * i : 128 * (i + 1)], words[:, 256 * a + u : 256 * (a + 1) : 2], ident[:])
            x_bank[g, half] = bank

        def words_out(g, half):
            t = tile_of(x_grouped, g, [P, 2048], BF16, name="x_grouped", align_bytes=64, bufs=2)
            copy_out(
                "X" + str(half),
                g,
                t[:].bitcast(F32)[:, 512 * half : 512 * (half + 1)].rearrange("p (r u) -> p r u", u=2),
                x_bank[g, half][:].rearrange("p u r -> p r u"),
            )

        def quantized(src, name):
            codes = work.tile([P, 512], U32, name=name + "_codes", align_bytes=64, bufs=3)
            scales = work.tile([P, 512], U8, name=name + "_scales", align_bytes=64, bufs=3)
            quantize((codes, scales), src)
            return codes, scales

        def multiply(out, lhs, lhs_cols, rhs, rhs_cols):
            nc.tensor.matmul_mx(
                out=out,
                lhsT=lhs[0][:, lhs_cols].bitcast(FP8X4),
                lhsT_scale=lhs[1][:, lhs_cols],
                rhs=rhs[0][:, rhs_cols].bitcast(FP8X4),
                rhs_scale=rhs[1][:, rhs_cols],
                start=True,
                stop=True,
            )

        def block(a):
            return slice(128 * a, 128 * (a + 1))

        def down(g, a):
            t = tile_of(d_grouped, g, [P, 2048], BF16, name="d_grouped", align_bytes=64, bufs=2)
            bank = ps_d.tile([P, 4, 128], F32, name="d_bank")
            for c in range(4):
                multiply(bank[:, c, :], wd, block(c), xq[g], block(a))
            copy_out(
                "D" + str(a),
                g,
                t[:, 512 * a : 512 * (a + 1)].rearrange("p (n t) -> p n t", t=4),
                bank[:].rearrange("p t n -> p n t"),
            )

        def rope_matmul(g):
            bank = ps_r.tile([P, 512], F32, name="r_bank")
            for a in range(4):
                multiply(bank[:, block(a)], xq[g], block(a), wr, slice(0, 128))
            r_bank[g] = bank

        def rope_cosines(g):
            t = tile_of(r_cos, g, [P, 2, 4, 64], F32, name="r_cos", bufs=2)
            nc.vector.tensor_tensor(
                out=t[:].rearrange("p h j (i o) -> p h j i o", o=2),
                in0=r_bank[g][:].rearrange("p (j h i o) -> p h j i o", j=4, h=2, o=2),
                in1=cos_rows[:, g // 2].rearrange("p (j i) -> p j i", j=4).unsqueeze(1).unsqueeze(4).to_broadcast([P, 2, 4, 32, 2]),
                op=MULT,
            )

        def rope_sines(g):
            if g == 0:
                rows = sin_rows[:].rearrange("p g (j i) -> p (g j) i", j=4)
                nc.vector.tensor_scalar(out=sin2[:, :, 0, :], in0=rows, scalar1=-1.0, scalar2=None, op0=MULT)
                nc.vector.tensor_copy(out=sin2[:, :, 1, :], in_=rows)
            t = tile_of(r_sin, g, [P, 2, 4, 64], F32, name="r_sin", bufs=2)
            first = 4 * (g // 2)
            for h in range(2):
                nc.vector.tensor_tensor(
                    out=t[:, h].rearrange("p j (i o) -> p j i o", o=2),
                    in0=r_bank[g][:].rearrange("p (j h i o) -> p h j i o", j=4, h=2, o=2)[:, h, :, :, ::-1],
                    in1=sin2[:, first : first + 4].rearrange("p j o i -> p j i o"),
                    op=MULT,
                )

        def keys_of(g):
            return tile_of(k_out, g, [P, 2, 4, 192], F32, name="k_out", bufs=3)

        def values_of(g):
            return tile_of(v_out, g, [P, 2, 4, 128], F32, name="v_out", bufs=3)

        def rope_sum(g):
            engine = nc.vector
            engine.tensor_tensor(out=keys_of(g)[:, :, :, 128:192], in0=r_cos[g][:], in1=r_sin[g][:], op=ADD)

        def up(g, i):
            half = i // 2
            first, dest = ((0, keys_of(g)), (256, values_of(g)))[i % 2]
            bank = ps_u.tile([P, 2, 256], F32, name="u_bank")
            for j in range(2):
                multiply(bank[:, j, :], dq[g], block(2 * half + j), wu, slice(first, first + 256))
            copy_out(
                "U" + str(i),
                g,
                dest[:, :, 2 * half : 2 * half + 2, 0:128].rearrange("p h j d -> p j h d"),
                bank[:].rearrange("p j (h d) -> p j h d", h=2),
            )

        def store(g):
            b, rows = rows_of(g)
            keys = out_0[b, :, rows, :].rearrange("h (p j) d -> p h j d", j=4)
            values = out_1[b, :, rows, :].rearrange("h (p j) d -> p h j d", j=4)
            parts = ((0, 4),) if g < GROUPS - 1 else ((0, 2), (2, 4))
            for lo, hi in parts:
                for dest, src in ((keys, k_out[g]), (values, v_out[g])):
                    nc.sync.dma_start(
                        out=dest[:, :, lo:hi, :].rearrange("p h j d -> p h (j d)"),
                        in_=src[:, :, lo:hi, :].rearrange("p h j d -> p h (j d)"),
                    )

        def quantize_x(g):
            if g == 0:
                quantize(wd, wd_grouped)
            xq[g] = quantized(x_grouped[g], "x")
            if g == 0:
                nc.vector.tensor_copy(out=wr_grouped[:].rearrange("p (c j) -> p c j", j=4), in_=wr_raw[:].rearrange("p j c -> p c j"))
                nc.vector.tensor_copy(out=wu_grouped[:, 1024:2048].rearrange("p (c j) -> p c j", j=4), in_=wv_raw[:].rearrange("p j c -> p c j"))
                quantize(wr, wr_grouped)

        def quantize_d(g):
            if g == 0:
                quantize(wu, wu_grouped)
            dq[g] = quantized(d_grouped[g], "d")

        nc.scalar.copy(out=scale2[:, 512:1024], in_=scale2[:, 0:512])
        nc.scalar.copy(out=wd_grouped[:].rearrange("p (t m j) -> p t m j", t=4, j=4), in_=wd_raw[:].rearrange("p j (m t) -> p t m j", t=4))
        nc.scalar.copy(out=wu_grouped[:, 0:1024].rearrange("p (c j) -> p c j", j=4), in_=wk_raw[:].rearrange("p j c -> p c j"))
        stages = {
            "LOAD": lambda g: load(g) if g > 2 else None,
            "Q1": quantize_x,
            "R": rope_matmul,
            "A": rope_cosines,
            "B": rope_sines,
            "AD": rope_sum,
            "Q2": quantize_d,
            "ST": store,
        }
        for i in range(4):
            stages["D" + str(i)] = lambda g, i=i: down(g, i)
            stages["U" + str(i)] = lambda g, i=i: up(g, i)
        for i in range(2):
            stages["P" + str(i)] = lambda g, i=i: product(g, i)
            stages["T" + str(i)] = lambda g, i=i: turn(g, i)
            stages["X" + str(i)] = lambda g, i=i: words_out(g, i)
        for f in range(-6, 19):
            for name, lag in FRAME:
                if 0 <= f - lag < GROUPS:
                    stages[name](f - lag)
